import numpy as np
import ml_dtypes


def mxq(x, axis, fmt="e4m3"):
    dtype, down = {"e4m3": (ml_dtypes.float8_e4m3fn, 7), "e5m2": (ml_dtypes.float8_e5m2, 14)}[fmt]
    v = np.moveaxis(np.asarray(x, np.float32).astype(ml_dtypes.bfloat16).astype(np.float64), axis, -1)
    blocks = v.reshape(v.shape[:-1] + (-1, 32))
    amax = np.abs(blocks).max(-1, keepdims=True)
    byte = np.maximum(np.where(amax > 0, np.frexp(amax)[1] - 1 + 127, 0) - down, 1)
    scale = np.exp2(byte - 127.0)
    codes = (blocks / scale).astype(np.float32).astype(dtype).astype(np.float64)
    return np.moveaxis((codes * scale).reshape(v.shape), -1, axis)


WIDE = False


def mx_kscale(k):
    if not WIDE:
        return np.ones(k)
    levels = np.array([10, -10, 5, -5, 0])
    a = np.random.permutation(np.resize(levels, k // 512 * 4)).reshape(k // 512, 4)
    idx = np.arange(k)
    return np.exp2(a[idx // 512, idx % 128 // 32])


BF16 = ml_dtypes.bfloat16


def bf(x):
    return np.asarray(x, np.float32).astype(BF16)


def f64(x):
    return np.asarray(x).astype(np.float64)


B, IN, H = 1024, 1024, 1024


def sigmoid(v):
    return 1.0 / (1.0 + np.exp(-v))


def setup_inputs():
    s = mx_kscale(IN)
    return {'input': bf(np.random.standard_normal((B, IN)) * s),
            'state': bf(np.random.standard_normal((B, H))),
            'c': bf(np.tanh(np.random.standard_normal((B, H)))),
            'W2': bf(np.random.standard_normal((IN, H)) * 0.7 / np.sqrt(IN) / s[:, None]),
            'U2': bf(np.random.standard_normal((H, H)) * 0.7 / np.sqrt(H)),
            'bias_gate': bf(np.random.standard_normal((1, H)) * 0.5)}


def reference(input, state, c, W2, U2, bias_gate):
    h = f64(state)
    wComp2 = mxq(f64(input), 1, 'e4m3') @ mxq(f64(W2), 0, 'e4m3')
    uComp2 = mxq(h, 1, 'e4m3') @ mxq(f64(U2), 0, 'e4m3')
    z = sigmoid(wComp2 + uComp2 + f64(bias_gate))
    return z * h + (1.0 - z) * f64(c)

@@ -1,0 +1,190 @@
+from contextlib import ExitStack
+
+import concourse.mybir as mybir
+from concourse.masks import make_identity
+
+F32 = mybir.dt.float32
+BF16 = mybir.dt.bfloat16
+U32 = mybir.dt.uint32
+U8 = mybir.dt.uint8
+FP8X4 = mybir.dt.float8_e4m3fn_x4
+ACT = mybir.ActivationFunctionType
+ALU = mybir.AluOpType
+
+P = 128
+ROWS = 1024
+FEATS = 1024
+PACK = 4
+K_PASS = P * PACK
+PASSES = 2 * FEATS // K_PASS
+HALF = 512
+HALVES = ROWS // HALF
+ROWS_PER_PART = HALF // P
+H_TILES = FEATS // P
+PAIR = 2
+
+FLOPS = 2 * ROWS * FEATS * 2 * FEATS
+
+
+def tile_grulrcell_pb_kernel(tc, x_in, state, cand, w2, u2, bias_gate, out):
+    nc = tc.nc
+    with ExitStack() as ctx:
+        keep = ctx.enter_context(tc.tile_pool(name="keep", bufs=1))
+        stage = ctx.enter_context(tc.tile_pool(name="stage", bufs=4))
+        gates = ctx.enter_context(tc.tile_pool(name="gates", bufs=H_TILES + 2))
+        blend = ctx.enter_context(tc.tile_pool(name="blend", bufs=3))
+        psum = ctx.enter_context(tc.psum_pool(name="psum", bufs=8))
+
+        def load_rows(src, half, name):
+            rows = keep.tile([P, ROWS_PER_PART, FEATS], BF16, name=name)
+            nc.sync.dma_start(
+                out=rows[:],
+                in_=src[HALF * half : HALF * (half + 1), :].rearrange("(p i) k -> p i k", i=ROWS_PER_PART),
+            )
+            return rows
+
+        def load_weights(src, g, name):
+            raw = keep.tile([P, PACK, FEATS], BF16, name=name)
+            nc.sync.dma_start(
+                out=raw[:].rearrange("p (u e) h -> p u e h", u=2),
+                in_=src[K_PASS * g : K_PASS * (g + 1), :].rearrange("(u p e) h -> p u e h", u=2, e=2),
+            )
+            return raw
+
+        bias_rows = keep.tile([H_TILES, P], BF16)
+        nc.sync.dma_start(out=bias_rows[:], in_=bias_gate.rearrange("o (j m) -> (o j) m", m=P))
+
+        x_rows = [load_rows(x_in, 0, "x_rows0")]
+        state_rows = [load_rows(state, 0, "state_rows0")]
+        x_rows.append(load_rows(x_in, 1, "x_rows1"))
+        state_rows.append(load_rows(state, 1, "state_rows1"))
+        raw_weights = [
+            load_weights(w2, 0, "raw_w2_0"),
+            load_weights(w2, 1, "raw_w2_1"),
+            load_weights(u2, 0, "raw_u2_0"),
+            load_weights(u2, 1, "raw_u2_1"),
+        ]
+        cand_rows = [load_rows(cand, 0, "cand_rows0"), load_rows(cand, 1, "cand_rows1")]
+
+        ident = keep.tile([P, P], F32)
+        make_identity(nc, ident[:])
+
+        warm = keep.tile([P, 1], F32)
+        nc.vector.memset(warm[:], 0.0)
+        nc.scalar.activation(out=warm[:], in_=warm[:], func=ACT.Sigmoid)
+
+        bias_square = keep.tile([P, P], F32)
+        nc.vector.memset(bias_square[:], 0.0)
+        nc.vector.tensor_copy(out=bias_square[0:H_TILES, :], in_=bias_rows[:])
+        bias_bank = psum.tile([P, HALF], F32, tag="bank")
+        nc.tensor.transpose(bias_bank[:, 0:P], bias_square[:], ident[:])
+        bias_col = keep.tile([P, H_TILES], F32)
+        nc.vector.tensor_copy(out=bias_col[:], in_=bias_bank[:, 0:H_TILES])
+
+        row_codes = keep.tile([P, PASSES, HALVES, HALF], U32, align_bytes=64)
+        row_scales = keep.tile([P, PASSES, HALVES, HALF], U8, align_bytes=64)
+        weight_codes = keep.tile([P, PASSES, FEATS], U32, align_bytes=64)
+        weight_scales = keep.tile([P, PASSES, FEATS], U8, align_bytes=64)
+
+        def quantise_rows(half):
+            for c in range(PASSES):
+                rows = (x_rows if c < 2 else state_rows)[half]
+                words_in = rows[:].bitcast(F32)
+                grouped = stage.tile([P, PACK * HALF], BF16, tag="grouped", align_bytes=64)
+                words_out = grouped[:].bitcast(F32).rearrange("q (n u) -> q n u", u=2)
+                for pair in range(2):
+                    bank = psum.tile([P, 2, 2 * P], F32, tag="bank")
+                    for u in range(2):
+                        for ii in range(2):
+                            first = (K_PASS // 2) * (c % 2) + P * u
+                            nc.tensor.transpose(
+                                bank[:, u, P * ii : P * (ii + 1)],
+                                words_in[:, 2 * pair + ii, first : first + P],
+                                ident[:],
+                            )
+                    nc.scalar.copy(
+                        out=words_out[:, 2 * P * pair : 2 * P * (pair + 1), :],
+                        in_=bank[:].rearrange("q u n -> q n u"),
+                    )
+                nc.vector.quantize_mx(
+                    out=row_codes[:, c, half, :].bitcast(FP8X4),
+                    scales=row_scales[:, c, half, :],
+                    in_=grouped[:],
+                )
+
+        def quantise_weights(c):
+            for part in range(2):
+                cols = slice(HALF * part, HALF * (part + 1))
+                grouped = stage.tile([P, PACK * HALF], BF16, tag="grouped", align_bytes=64)
+                dst = grouped[:].rearrange("p (a i t) -> p a t i", i=4, t=PACK)
+                src = raw_weights[c][:, :, cols].rearrange("p t (a i) -> p a t i", i=4)
+                if part == 0:
+                    nc.vector.tensor_copy(out=dst, in_=src)
+                else:
+                    nc.scalar.copy(out=dst, in_=src)
+                nc.vector.quantize_mx(
+                    out=weight_codes[:, c, cols].bitcast(FP8X4),
+                    scales=weight_scales[:, c, cols],
+                    in_=grouped[:],
+                )
+
+        def mx_pass(acc, c, half, j):
+            h_cols = slice(P * j, P * (j + 1))
+            nc.tensor.matmul_mx(
+                out=acc[:],
+                lhsT=weight_codes[:, c, h_cols].bitcast(FP8X4),
+                lhsT_scale=weight_scales[:, c, h_cols],
+                rhs=row_codes[:, c, half, :].bitcast(FP8X4),
+                rhs_scale=row_scales[:, c, half, :],
+                start=(c == 0),
+                stop=(c == PASSES - 1),
+            )
+
+        def gate(acc, j):
+            z_t = gates.tile([P, HALF], F32, tag="z_t")
+            nc.scalar.activation(out=z_t[:], in_=acc[:], func=ACT.Sigmoid, bias=bias_col[:, j : j + 1], scale=1.0)
+            return z_t
+
+        def blend_tile(z_t, half, j, result):
+            z = psum.tile([P, ROWS_PER_PART, P], F32, tag="bank")
+            for i in range(ROWS_PER_PART):
+                nc.tensor.transpose(z[:, i, :], z_t[:, P * i : P * (i + 1)], ident[:])
+            h_cols = slice(P * j, P * (j + 1))
+            kept = blend.tile([P, ROWS_PER_PART, P], F32, tag="kept")
+            nc.vector.tensor_tensor(out=kept[:], in0=z[:], in1=state_rows[half][:, :, h_cols], op=ALU.mult)
+            fresh = blend.tile([P, ROWS_PER_PART, P], F32, tag="fresh")
+            nc.vector.scalar_tensor_tensor(
+                out=fresh[:], in0=z[:], scalar=-1.0, in1=cand_rows[half][:, :, h_cols], op0=ALU.add, op1=ALU.mult
+            )
+            nc.gpsimd.tensor_tensor(out=result, in0=kept[:], in1=fresh[:], op=ALU.subtract)
+
+        quantise_rows(0)
+        quantise_rows(1)
+
+        first_acc = []
+        for j in range(H_TILES):
+            first_acc.append(psum.tile([P, HALF], F32, tag="bank", name="first_acc%d" % j))
+        for c in range(PASSES):
+            quantise_weights(c)
+            for j in range(H_TILES):
+                mx_pass(first_acc[j], c, 0, j)
+        waiting = []
+        for j in range(H_TILES):
+            waiting.append((gate(first_acc[j], j), 0, j))
+
+        for r in range(H_TILES):
+            acc = psum.tile([P, HALF], F32, tag="bank")
+            for c in range(PASSES):
+                mx_pass(acc, c, 1, r)
+            waiting.append((gate(acc, r), 1, r))
+            result = blend.tile([P, ROWS_PER_PART, PAIR * P], F32, tag="result")
+            for k in range(PAIR):
+                z_t, half, j = waiting[PAIR * r + k]
+                blend_tile(z_t, half, j, result[:, :, P * k : P * (k + 1)])
+            z_t, half, j = waiting[PAIR * r]
+            nc.sync.dma_start(
+                out=out[HALF * half : HALF * (half + 1), P * j : P * (j + PAIR)].rearrange(
+                    "(p i) h -> p i h", i=ROWS_PER_PART
+                ),
+                in_=result[:],
+            )

@@ -56,15 +56,16 @@ def tile_grulrcell_pb_kernel(tc, x_in, state, cand, w2, u2, bias_gate, out):
 
         x_rows = [load_rows(x_in, 0, "x_rows0")]
         state_rows = [load_rows(state, 0, "state_rows0")]
-        x_rows.append(load_rows(x_in, 1, "x_rows1"))
-        state_rows.append(load_rows(state, 1, "state_rows1"))
         raw_weights = [
             load_weights(w2, 0, "raw_w2_0"),
             load_weights(w2, 1, "raw_w2_1"),
             load_weights(u2, 0, "raw_u2_0"),
             load_weights(u2, 1, "raw_u2_1"),
         ]
-        cand_rows = [load_rows(cand, 0, "cand_rows0"), load_rows(cand, 1, "cand_rows1")]
+        cand_rows = [load_rows(cand, 0, "cand_rows0")]
+        x_rows.append(load_rows(x_in, 1, "x_rows1"))
+        state_rows.append(load_rows(state, 1, "state_rows1"))
+        cand_rows.append(load_rows(cand, 1, "cand_rows1"))
 
         ident = keep.tile([P, P], F32)
         make_identity(nc, ident[:])
@@ -86,31 +87,30 @@ def tile_grulrcell_pb_kernel(tc, x_in, state, cand, w2, u2, bias_gate, out):
         weight_codes = keep.tile([P, PASSES, FEATS], U32, align_bytes=64)
         weight_scales = keep.tile([P, PASSES, FEATS], U8, align_bytes=64)
 
-        def quantise_rows(half):
-            for c in range(PASSES):
-                rows = (x_rows if c < 2 else state_rows)[half]
-                words_in = rows[:].bitcast(F32)
-                grouped = stage.tile([P, PACK * HALF], BF16, tag="grouped", align_bytes=64)
-                words_out = grouped[:].bitcast(F32).rearrange("q (n u) -> q n u", u=2)
-                for pair in range(2):
-                    bank = psum.tile([P, 2, 2 * P], F32, tag="bank")
-                    for u in range(2):
-                        for ii in range(2):
-                            first = (K_PASS // 2) * (c % 2) + P * u
-                            nc.tensor.transpose(
-                                bank[:, u, P * ii : P * (ii + 1)],
-                                words_in[:, 2 * pair + ii, first : first + P],
-                                ident[:],
-                            )
-                    nc.scalar.copy(
-                        out=words_out[:, 2 * P * pair : 2 * P * (pair + 1), :],
-                        in_=bank[:].rearrange("q u n -> q n u"),
-                    )
-                nc.vector.quantize_mx(
-                    out=row_codes[:, c, half, :].bitcast(FP8X4),
-                    scales=row_scales[:, c, half, :],
-                    in_=grouped[:],
+        def quantise_rows(half, c):
+            rows = (x_rows if c < 2 else state_rows)[half]
+            words_in = rows[:].bitcast(F32)
+            grouped = stage.tile([P, PACK * HALF], BF16, tag="grouped", align_bytes=64)
+            words_out = grouped[:].bitcast(F32).rearrange("q (n u) -> q n u", u=2)
+            for pair in range(2):
+                bank = psum.tile([P, 2, 2 * P], F32, tag="bank")
+                for u in range(2):
+                    for ii in range(2):
+                        first = (K_PASS // 2) * (c % 2) + P * u
+                        nc.tensor.transpose(
+                            bank[:, u, P * ii : P * (ii + 1)],
+                            words_in[:, 2 * pair + ii, first : first + P],
+                            ident[:],
+                        )
+                nc.scalar.copy(
+                    out=words_out[:, 2 * P * pair : 2 * P * (pair + 1), :],
+                    in_=bank[:].rearrange("q u n -> q n u"),
                 )
+            nc.vector.quantize_mx(
+                out=row_codes[:, c, half, :].bitcast(FP8X4),
+                scales=row_scales[:, c, half, :],
+                in_=grouped[:],
+            )
 
         def quantise_weights(c):
             for part in range(2):
@@ -158,8 +158,8 @@ def tile_grulrcell_pb_kernel(tc, x_in, state, cand, w2, u2, bias_gate, out):
             )
             nc.gpsimd.tensor_tensor(out=result, in0=kept[:], in1=fresh[:], op=ALU.subtract)
 
-        quantise_rows(0)
-        quantise_rows(1)
+        for c in range(PASSES):
+            quantise_rows(0, c)
 
         first_acc = []
         for j in range(H_TILES):
@@ -168,23 +168,34 @@ def tile_grulrcell_pb_kernel(tc, x_in, state, cand, w2, u2, bias_gate, out):
             quantise_weights(c)
             for j in range(H_TILES):
                 mx_pass(first_acc[j], c, 0, j)
-        waiting = []
-        for j in range(H_TILES):
-            waiting.append((gate(first_acc[j], j), 0, j))
-
-        for r in range(H_TILES):
-            acc = psum.tile([P, HALF], F32, tag="bank")
-            for c in range(PASSES):
-                mx_pass(acc, c, 1, r)
-            waiting.append((gate(acc, r), 1, r))
+        def blend_pair(z_pair, half, j):
             result = blend.tile([P, ROWS_PER_PART, PAIR * P], F32, tag="result")
             for k in range(PAIR):
-                z_t, half, j = waiting[PAIR * r + k]
-                blend_tile(z_t, half, j, result[:, :, P * k : P * (k + 1)])
-            z_t, half, j = waiting[PAIR * r]
+                blend_tile(z_pair[k], half, j + k, result[:, :, P * k : P * (k + 1)])
             nc.sync.dma_start(
                 out=out[HALF * half : HALF * (half + 1), P * j : P * (j + PAIR)].rearrange(
                     "(p i) h -> p i h", i=ROWS_PER_PART
                 ),
                 in_=result[:],
             )
+
+        first_z = [gate(first_acc[j], j) for j in range(H_TILES)]
+
+        blend_pair(first_z[0:2], 0, 0)
+        quantise_rows(1, 0)
+        quantise_rows(1, 1)
+        blend_pair(first_z[2:4], 0, 2)
+        quantise_rows(1, 2)
+        quantise_rows(1, 3)
+        blend_pair(first_z[4:6], 0, 4)
+        blend_pair(first_z[6:8], 0, 6)
+
+        second_z = []
+        for j in range(H_TILES):
+            acc = psum.tile([P, HALF], F32, tag="bank")
+            for c in range(PASSES):
+                mx_pass(acc, c, 1, j)
+            second_z.append(gate(acc, j))
+            if j % PAIR == 1 and j >= 2 * PAIR - 1:
+                blend_pair(second_z[j - 3 : j - 1], 1, j - 3)
+        blend_pair(second_z[H_TILES - PAIR : H_TILES], 1, H_TILES - PAIR)

@@ -37,10 +37,9 @@ def tile_grulrcell_pb_kernel(tc, x_in, state, cand, w2, u2, bias_gate, out):
 
         def load_rows(src, half, name):
             rows = keep.tile([P, ROWS_PER_PART, FEATS], BF16, name=name)
-            nc.sync.dma_start(
-                out=rows[:],
-                in_=src[HALF * half : HALF * (half + 1), :].rearrange("(p i) k -> p i k", i=ROWS_PER_PART),
-            )
+            view = src[HALF * half : HALF * (half + 1), :].rearrange("(p i) k -> p i k", i=ROWS_PER_PART)
+            for two in range(2):
+                nc.sync.dma_start(out=rows[:, 2 * two : 2 * two + 2, :], in_=view[:, 2 * two : 2 * two + 2, :])
             return rows
 
         def load_weights(src, g, name):
@@ -87,30 +86,33 @@ def tile_grulrcell_pb_kernel(tc, x_in, state, cand, w2, u2, bias_gate, out):
         weight_codes = keep.tile([P, PASSES, FEATS], U32, align_bytes=64)
         weight_scales = keep.tile([P, PASSES, FEATS], U8, align_bytes=64)
 
-        def quantise_rows(half, c):
-            rows = (x_rows if c < 2 else state_rows)[half]
+        def quantise_rows(half, rows, first_pass):
             words_in = rows[:].bitcast(F32)
-            grouped = stage.tile([P, PACK * HALF], BF16, tag="grouped", align_bytes=64)
-            words_out = grouped[:].bitcast(F32).rearrange("q (n u) -> q n u", u=2)
-            for pair in range(2):
-                bank = psum.tile([P, 2, 2 * P], F32, tag="bank")
-                for u in range(2):
-                    for ii in range(2):
-                        first = (K_PASS // 2) * (c % 2) + P * u
-                        nc.tensor.transpose(
-                            bank[:, u, P * ii : P * (ii + 1)],
-                            words_in[:, 2 * pair + ii, first : first + P],
-                            ident[:],
-                        )
-                nc.scalar.copy(
-                    out=words_out[:, 2 * P * pair : 2 * P * (pair + 1), :],
-                    in_=bank[:].rearrange("q u n -> q n u"),
+            grouped = []
+            for g in range(2):
+                grouped.append(stage.tile([P, PACK * HALF], BF16, tag="grouped", name="grouped%d" % g, align_bytes=64))
+            for two in range(2):
+                for g in range(2):
+                    bank = psum.tile([P, 2, 2 * P], F32, tag="bank")
+                    for u in range(2):
+                        for ii in range(2):
+                            first = (K_PASS // 2) * g + P * u
+                            nc.tensor.transpose(
+                                bank[:, u, P * ii : P * (ii + 1)],
+                                words_in[:, 2 * two + ii, first : first + P],
+                                ident[:],
+                            )
+                    words_out = grouped[g][:].bitcast(F32).rearrange("q (n u) -> q n u", u=2)
+                    nc.scalar.copy(
+                        out=words_out[:, 2 * P * two : 2 * P * (two + 1), :],
+                        in_=bank[:].rearrange("q u n -> q n u"),
+                    )
+            for g in range(2):
+                nc.vector.quantize_mx(
+                    out=row_codes[:, first_pass + g, half, :].bitcast(FP8X4),
+                    scales=row_scales[:, first_pass + g, half, :],
+                    in_=grouped[g][:],
                 )
-            nc.vector.quantize_mx(
-                out=row_codes[:, c, half, :].bitcast(FP8X4),
-                scales=row_scales[:, c, half, :],
-                in_=grouped[:],
-            )
 
         def quantise_weights(c):
             for part in range(2):
@@ -158,8 +160,8 @@ def tile_grulrcell_pb_kernel(tc, x_in, state, cand, w2, u2, bias_gate, out):
             )
             nc.gpsimd.tensor_tensor(out=result, in0=kept[:], in1=fresh[:], op=ALU.subtract)
 
-        for c in range(PASSES):
-            quantise_rows(0, c)
+        quantise_rows(0, x_rows[0], 0)
+        quantise_rows(0, state_rows[0], 2)
 
         first_acc = []
         for j in range(H_TILES):
@@ -182,11 +184,9 @@ def tile_grulrcell_pb_kernel(tc, x_in, state, cand, w2, u2, bias_gate, out):
         first_z = [gate(first_acc[j], j) for j in range(H_TILES)]
 
         blend_pair(first_z[0:2], 0, 0)
-        quantise_rows(1, 0)
-        quantise_rows(1, 1)
+        quantise_rows(1, x_rows[1], 0)
         blend_pair(first_z[2:4], 0, 2)
-        quantise_rows(1, 2)
-        quantise_rows(1, 3)
+        quantise_rows(1, state_rows[1], 2)
         blend_pair(first_z[4:6], 0, 4)
         blend_pair(first_z[6:8], 0, 6)
 

@@ -147,7 +147,7 @@ def tile_grulrcell_pb_kernel(tc, x_in, state, cand, w2, u2, bias_gate, out):
             nc.scalar.activation(out=z_t[:], in_=acc[:], func=ACT.Sigmoid, bias=bias_col[:, j : j + 1], scale=1.0)
             return z_t
 
-        def blend_tile(z_t, half, j, result):
+        def blend_tile(z_t, half, j, result, last_engine):
             z = psum.tile([P, ROWS_PER_PART, P], F32, tag="bank")
             for i in range(ROWS_PER_PART):
                 nc.tensor.transpose(z[:, i, :], z_t[:, P * i : P * (i + 1)], ident[:])
@@ -158,7 +158,7 @@ def tile_grulrcell_pb_kernel(tc, x_in, state, cand, w2, u2, bias_gate, out):
             nc.vector.scalar_tensor_tensor(
                 out=fresh[:], in0=z[:], scalar=-1.0, in1=cand_rows[half][:, :, h_cols], op0=ALU.add, op1=ALU.mult
             )
-            nc.gpsimd.tensor_tensor(out=result, in0=kept[:], in1=fresh[:], op=ALU.subtract)
+            last_engine.tensor_tensor(out=result, in0=kept[:], in1=fresh[:], op=ALU.subtract)
 
         quantise_rows(0, x_rows[0], 0)
         quantise_rows(0, state_rows[0], 2)
@@ -173,9 +173,19 @@ def tile_grulrcell_pb_kernel(tc, x_in, state, cand, w2, u2, bias_gate, out):
         def blend_pair(z_pair, half, j):
             result = blend.tile([P, ROWS_PER_PART, PAIR * P], F32, tag="result")
             for k in range(PAIR):
-                blend_tile(z_pair[k], half, j + k, result[:, :, P * k : P * (k + 1)])
+                blend_tile(z_pair[k], half, j + k, result[:, :, P * k : P * (k + 1)], nc.gpsimd)
             nc.sync.dma_start(
                 out=out[HALF * half : HALF * (half + 1), P * j : P * (j + PAIR)].rearrange(
+                    "(p i) h -> p i h", i=ROWS_PER_PART
+                ),
+                in_=result[:],
+            )
+
+        def blend_single(z_t, half, j):
+            result = blend.tile([P, ROWS_PER_PART, P], F32, tag="single")
+            blend_tile(z_t, half, j, result[:], nc.vector)
+            nc.sync.dma_start(
+                out=out[HALF * half : HALF * (half + 1), P * j : P * (j + 1)].rearrange(
                     "(p i) h -> p i h", i=ROWS_PER_PART
                 ),
                 in_=result[:],
@@ -198,4 +208,5 @@ def tile_grulrcell_pb_kernel(tc, x_in, state, cand, w2, u2, bias_gate, out):
             second_z.append(gate(acc, j))
             if j % PAIR == 1 and j >= 2 * PAIR - 1:
                 blend_pair(second_z[j - 3 : j - 1], 1, j - 3)
-        blend_pair(second_z[H_TILES - PAIR : H_TILES], 1, H_TILES - PAIR)
+        for j in range(H_TILES - PAIR, H_TILES):
+            blend_single(second_z[j], 1, j)

@@ -21,6 +21,7 @@ HALF = 512
 HALVES = ROWS // HALF
 ROWS_PER_PART = HALF // P
 H_TILES = FEATS // P
+SPAN_TILES = (1, 2, 3)
 PAIR = 2
 
 FLOPS = 2 * ROWS * FEATS * 2 * FEATS
@@ -32,7 +33,7 @@ def tile_grulrcell_pb_kernel(tc, x_in, state, cand, w2, u2, bias_gate, out):
         keep = ctx.enter_context(tc.tile_pool(name="keep", bufs=1))
         stage = ctx.enter_context(tc.tile_pool(name="stage", bufs=4))
         gates = ctx.enter_context(tc.tile_pool(name="gates", bufs=H_TILES + 2))
-        blend = ctx.enter_context(tc.tile_pool(name="blend", bufs=3))
+        blend = ctx.enter_context(tc.tile_pool(name="blend", bufs=4))
         psum = ctx.enter_context(tc.psum_pool(name="psum", bufs=8))
 
         def load_rows(src, half, name):
@@ -153,6 +154,10 @@ def tile_grulrcell_pb_kernel(tc, x_in, state, cand, w2, u2, bias_gate, out):
                 nc.tensor.transpose(z[:, i, :], z_t[:, P * i : P * (i + 1)], ident[:])
             h_cols = slice(P * j, P * (j + 1))
             kept = blend.tile([P, ROWS_PER_PART, P], F32, tag="kept")
+            if (half, j) in spans:
+                nc.vector.tensor_tensor(out=kept[:], in0=z[:], in1=spans[half, j][:], op=ALU.mult)
+                last_engine.tensor_tensor(out=result, in0=kept[:], in1=cand_rows[half][:, :, h_cols], op=ALU.add)
+                return
             nc.vector.tensor_tensor(out=kept[:], in0=z[:], in1=state_rows[half][:, :, h_cols], op=ALU.mult)
             fresh = blend.tile([P, ROWS_PER_PART, P], F32, tag="fresh")
             nc.vector.scalar_tensor_tensor(
@@ -162,6 +167,15 @@ def tile_grulrcell_pb_kernel(tc, x_in, state, cand, w2, u2, bias_gate, out):
 
         quantise_rows(0, x_rows[0], 0)
         quantise_rows(0, state_rows[0], 2)
+
+        spans = {}
+        for j in SPAN_TILES:
+            h_cols = slice(P * j, P * (j + 1))
+            span = keep.tile([P, ROWS_PER_PART, P], F32, name="span%d" % j)
+            nc.gpsimd.tensor_tensor(
+                out=span[:], in0=state_rows[0][:, :, h_cols], in1=cand_rows[0][:, :, h_cols], op=ALU.subtract
+            )
+            spans[0, j] = span
 
         first_acc = []
         for j in range(H_TILES):

@@ -131,14 +131,14 @@ def tile_grulrcell_pb_kernel(tc, x_in, state, cand, w2, u2, bias_gate, out):
                     in_=grouped[:],
                 )
 
-        def mx_pass(acc, c, half, j):
+        def mx_pass(acc, c, half, j, cols=slice(0, HALF)):
             h_cols = slice(P * j, P * (j + 1))
             nc.tensor.matmul_mx(
                 out=acc[:],
                 lhsT=weight_codes[:, c, h_cols].bitcast(FP8X4),
                 lhsT_scale=weight_scales[:, c, h_cols],
-                rhs=row_codes[:, c, half, :].bitcast(FP8X4),
-                rhs_scale=row_scales[:, c, half, :],
+                rhs=row_codes[:, c, half, cols].bitcast(FP8X4),
+                rhs_scale=row_scales[:, c, half, cols],
                 start=(c == 0),
                 stop=(c == PASSES - 1),
             )
@@ -214,13 +214,41 @@ def tile_grulrcell_pb_kernel(tc, x_in, state, cand, w2, u2, bias_gate, out):
         blend_pair(first_z[4:6], 0, 4)
         blend_pair(first_z[6:8], 0, 6)
 
+        def last_part(part):
+            j = H_TILES - 1
+            h_cols = slice(P * j, P * (j + 1))
+            rows = slice(2 * part, 2 * part + 2)
+            part_acc = psum.tile([P, 2 * P], F32, tag="bank")
+            for c in range(PASSES):
+                mx_pass(part_acc, c, 1, j, slice(2 * P * part, 2 * P * (part + 1)))
+            z_part = gates.tile([P, 2 * P], F32, tag="z_part")
+            nc.scalar.activation(
+                out=z_part[:], in_=part_acc[:], func=ACT.Sigmoid, bias=bias_col[:, j : j + 1], scale=1.0
+            )
+            z = psum.tile([P, 2, P], F32, tag="bank")
+            for i in range(2):
+                nc.tensor.transpose(z[:, i, :], z_part[:, P * i : P * (i + 1)], ident[:])
+            kept = blend.tile([P, 2, P], F32, tag="kept")
+            nc.vector.tensor_tensor(out=kept[:], in0=z[:], in1=state_rows[1][:, rows, h_cols], op=ALU.mult)
+            fresh = blend.tile([P, 2, P], F32, tag="fresh")
+            nc.vector.scalar_tensor_tensor(
+                out=fresh[:], in0=z[:], scalar=-1.0, in1=cand_rows[1][:, rows, h_cols], op0=ALU.add, op1=ALU.mult
+            )
+            result = blend.tile([P, 2, P], F32, tag="part")
+            nc.vector.tensor_tensor(out=result[:], in0=kept[:], in1=fresh[:], op=ALU.subtract)
+            nc.sync.dma_start(
+                out=out[HALF:ROWS, h_cols].rearrange("(p i) h -> p i h", i=ROWS_PER_PART)[:, rows, :], in_=result[:]
+            )
+
         second_z = []
-        for j in range(H_TILES):
+        for j in range(H_TILES - 1):
             acc = psum.tile([P, HALF], F32, tag="bank")
             for c in range(PASSES):
                 mx_pass(acc, c, 1, j)
             second_z.append(gate(acc, j))
             if j % PAIR == 1 and j >= 2 * PAIR - 1:
                 blend_pair(second_z[j - 3 : j - 1], 1, j - 3)
-        for j in range(H_TILES - PAIR, H_TILES):
-            blend_single(second_z[j], 1, j)
+        blend_pair(second_z[H_TILES - 2 * PAIR : H_TILES - PAIR], 1, H_TILES - 2 * PAIR)
+        blend_single(second_z[H_TILES - 2], 1, H_TILES - 2)
+        for part in range(2):
+            last_part(part)

@@ -52,7 +52,7 @@ def tile_grulrcell_pb_kernel(tc, x_in, state, cand, w2, u2, bias_gate, out):
             return raw
 
         bias_rows = keep.tile([H_TILES, P], BF16)
-        nc.sync.dma_start(out=bias_rows[:], in_=bias_gate.rearrange("o (j m) -> (o j) m", m=P))
+        nc.scalar.dma_start(out=bias_rows[:], in_=bias_gate.rearrange("o (j m) -> (o j) m", m=P))
 
         x_rows = [load_rows(x_in, 0, "x_rows0")]
         state_rows = [load_rows(state, 0, "state_rows0")]
@@ -82,10 +82,10 @@ def tile_grulrcell_pb_kernel(tc, x_in, state, cand, w2, u2, bias_gate, out):
         bias_col = keep.tile([P, H_TILES], F32)
         nc.vector.tensor_copy(out=bias_col[:], in_=bias_bank[:, 0:H_TILES])
 
-        row_codes = keep.tile([P, PASSES, HALVES, HALF], U32, align_bytes=64)
-        row_scales = keep.tile([P, PASSES, HALVES, HALF], U8, align_bytes=64)
-        weight_codes = keep.tile([P, PASSES, FEATS], U32, align_bytes=64)
-        weight_scales = keep.tile([P, PASSES, FEATS], U8, align_bytes=64)
+        row_codes = keep.tile([P, PASSES, HALVES, HALF], U32, align_bytes=256)
+        row_scales = keep.tile([P, PASSES, HALVES, HALF], U8, align_bytes=256)
+        weight_codes = keep.tile([P, PASSES, FEATS], U32, align_bytes=256)
+        weight_scales = keep.tile([P, PASSES, FEATS], U8, align_bytes=256)
 
         def quantise_rows(half, rows, first_pass):
             words_in = rows[:].bitcast(F32)

@@ -22,6 +22,7 @@ HALVES = ROWS // HALF
 ROWS_PER_PART = HALF // P
 H_TILES = FEATS // P
 SPAN_TILES = (1, 2, 3)
+EARLY = 4
 PAIR = 2
 
 FLOPS = 2 * ROWS * FEATS * 2 * FEATS
@@ -55,9 +56,9 @@ def tile_grulrcell_pb_kernel(tc, x_in, state, cand, w2, u2, bias_gate, out):
         nc.scalar.dma_start(out=bias_rows[:], in_=bias_gate.rearrange("o (j m) -> (o j) m", m=P))
 
         x_rows = [load_rows(x_in, 0, "x_rows0")]
+        raw_weights = [load_weights(w2, 0, "raw_w2_0")]
         state_rows = [load_rows(state, 0, "state_rows0")]
-        raw_weights = [
-            load_weights(w2, 0, "raw_w2_0"),
+        raw_weights += [
             load_weights(w2, 1, "raw_w2_1"),
             load_weights(u2, 0, "raw_u2_0"),
             load_weights(u2, 1, "raw_u2_1"),
@@ -165,7 +166,9 @@ def tile_grulrcell_pb_kernel(tc, x_in, state, cand, w2, u2, bias_gate, out):
             )
             last_engine.tensor_tensor(out=result, in0=kept[:], in1=fresh[:], op=ALU.subtract)
 
+        quantise_weights(0)
         quantise_rows(0, x_rows[0], 0)
+        quantise_weights(1)
         quantise_rows(0, state_rows[0], 2)
 
         spans = {}
@@ -181,7 +184,8 @@ def tile_grulrcell_pb_kernel(tc, x_in, state, cand, w2, u2, bias_gate, out):
         for j in range(H_TILES):
             first_acc.append(psum.tile([P, HALF], F32, tag="bank", name="first_acc%d" % j))
         for c in range(PASSES):
-            quantise_weights(c)
+            if c >= 2:
+                quantise_weights(c)
             for j in range(H_TILES):
                 mx_pass(first_acc[j], c, 0, j)
         def blend_pair(z_pair, half, j):
@@ -195,9 +199,9 @@ def tile_grulrcell_pb_kernel(tc, x_in, state, cand, w2, u2, bias_gate, out):
                 in_=result[:],
             )
 
-        def blend_single(z_t, half, j):
+        def blend_single(z_t, half, j, last_engine):
             result = blend.tile([P, ROWS_PER_PART, P], F32, tag="single")
-            blend_tile(z_t, half, j, result[:], nc.vector)
+            blend_tile(z_t, half, j, result[:], last_engine)
             nc.sync.dma_start(
                 out=out[HALF * half : HALF * (half + 1), P * j : P * (j + 1)].rearrange(
                     "(p i) h -> p i h", i=ROWS_PER_PART
@@ -208,16 +212,14 @@ def tile_grulrcell_pb_kernel(tc, x_in, state, cand, w2, u2, bias_gate, out):
         first_z = [gate(first_acc[j], j) for j in range(H_TILES)]
 
         blend_pair(first_z[0:2], 0, 0)
-        quantise_rows(1, x_rows[1], 0)
         blend_pair(first_z[2:4], 0, 2)
-        quantise_rows(1, state_rows[1], 2)
+        quantise_rows(1, x_rows[1], 0)
         blend_pair(first_z[4:6], 0, 4)
+        quantise_rows(1, state_rows[1], 2)
         blend_pair(first_z[6:8], 0, 6)
 
-        def last_part(part):
+        def last_gate(part):
             j = H_TILES - 1
-            h_cols = slice(P * j, P * (j + 1))
-            rows = slice(2 * part, 2 * part + 2)
             part_acc = psum.tile([P, 2 * P], F32, tag="bank")
             for c in range(PASSES):
                 mx_pass(part_acc, c, 1, j, slice(2 * P * part, 2 * P * (part + 1)))
@@ -225,30 +227,48 @@ def tile_grulrcell_pb_kernel(tc, x_in, state, cand, w2, u2, bias_gate, out):
             nc.scalar.activation(
                 out=z_part[:], in_=part_acc[:], func=ACT.Sigmoid, bias=bias_col[:, j : j + 1], scale=1.0
             )
+            return z_part
+
+        def last_blend(z_part, part):
+            h_cols = slice(P * (H_TILES - 1), P * H_TILES)
+            rows = slice(2 * part, 2 * part + 2)
             z = psum.tile([P, 2, P], F32, tag="bank")
             for i in range(2):
                 nc.tensor.transpose(z[:, i, :], z_part[:, P * i : P * (i + 1)], ident[:])
             kept = blend.tile([P, 2, P], F32, tag="kept")
-            nc.vector.tensor_tensor(out=kept[:], in0=z[:], in1=state_rows[1][:, rows, h_cols], op=ALU.mult)
-            fresh = blend.tile([P, 2, P], F32, tag="fresh")
-            nc.vector.scalar_tensor_tensor(
-                out=fresh[:], in0=z[:], scalar=-1.0, in1=cand_rows[1][:, rows, h_cols], op0=ALU.add, op1=ALU.mult
-            )
+            nc.vector.tensor_tensor(out=kept[:], in0=z[:], in1=last_span[:, rows, :], op=ALU.mult)
             result = blend.tile([P, 2, P], F32, tag="part")
-            nc.vector.tensor_tensor(out=result[:], in0=kept[:], in1=fresh[:], op=ALU.subtract)
+            nc.vector.tensor_tensor(out=result[:], in0=kept[:], in1=cand_rows[1][:, rows, h_cols], op=ALU.add)
             nc.sync.dma_start(
                 out=out[HALF:ROWS, h_cols].rearrange("(p i) h -> p i h", i=ROWS_PER_PART)[:, rows, :], in_=result[:]
             )
 
         second_z = []
+        early_acc = []
+        for j in range(EARLY):
+            early_acc.append(psum.tile([P, HALF], F32, tag="bank", name="early_acc%d" % j))
+            for c in range(2):
+                mx_pass(early_acc[j], c, 1, j)
         for j in range(H_TILES - 1):
-            acc = psum.tile([P, HALF], F32, tag="bank")
-            for c in range(PASSES):
+            if j < EARLY:
+                acc = early_acc[j]
+                passes = range(2, PASSES)
+            else:
+                acc = psum.tile([P, HALF], F32, tag="bank")
+                passes = range(PASSES)
+            for c in passes:
                 mx_pass(acc, c, 1, j)
             second_z.append(gate(acc, j))
             if j % PAIR == 1 and j >= 2 * PAIR - 1:
                 blend_pair(second_z[j - 3 : j - 1], 1, j - 3)
-        blend_pair(second_z[H_TILES - 2 * PAIR : H_TILES - PAIR], 1, H_TILES - 2 * PAIR)
-        blend_single(second_z[H_TILES - 2], 1, H_TILES - 2)
+        for j in range(H_TILES - 2 * PAIR, H_TILES - PAIR):
+            blend_single(second_z[j], 1, j, nc.gpsimd)
+        last_cols = slice(P * (H_TILES - 1), P * H_TILES)
+        last_span = keep.tile([P, ROWS_PER_PART, P], F32)
+        nc.vector.tensor_tensor(
+            out=last_span[:], in0=state_rows[1][:, :, last_cols], in1=cand_rows[1][:, :, last_cols], op=ALU.subtract
+        )
+        last_z = [last_gate(part) for part in range(2)]
+        blend_single(second_z[H_TILES - 2], 1, H_TILES - 2, nc.vector)
         for part in range(2):
-            last_part(part)
+            last_blend(last_z[part], part)

from contextlib import ExitStack

import concourse.mybir as mybir
from concourse.masks import make_identity

F32 = mybir.dt.float32
BF16 = mybir.dt.bfloat16
U32 = mybir.dt.uint32
U8 = mybir.dt.uint8
FP8X4 = mybir.dt.float8_e4m3fn_x4
ACT = mybir.ActivationFunctionType
ALU = mybir.AluOpType

P = 128
ROWS = 1024
FEATS = 1024
PACK = 4
K_PASS = P * PACK
PASSES = 2 * FEATS // K_PASS
HALF = 512
HALVES = ROWS // HALF
ROWS_PER_PART = HALF // P
H_TILES = FEATS // P
SPAN_TILES = (1, 2, 3)
EARLY = 4
PAIR = 2

FLOPS = 2 * ROWS * FEATS * 2 * FEATS


def tile_grulrcell_pb_kernel(tc, x_in, state, cand, w2, u2, bias_gate, out):
    nc = tc.nc
    with ExitStack() as ctx:
        keep = ctx.enter_context(tc.tile_pool(name="keep", bufs=1))
        stage = ctx.enter_context(tc.tile_pool(name="stage", bufs=4))
        gates = ctx.enter_context(tc.tile_pool(name="gates", bufs=H_TILES + 2))
        blend = ctx.enter_context(tc.tile_pool(name="blend", bufs=4))
        psum = ctx.enter_context(tc.psum_pool(name="psum", bufs=8))

        def load_rows(src, half, name):
            rows = keep.tile([P, ROWS_PER_PART, FEATS], BF16, name=name)
            view = src[HALF * half : HALF * (half + 1), :].rearrange("(p i) k -> p i k", i=ROWS_PER_PART)
            for two in range(2):
                nc.sync.dma_start(out=rows[:, 2 * two : 2 * two + 2, :], in_=view[:, 2 * two : 2 * two + 2, :])
            return rows

        def load_weights(src, g, name):
            raw = keep.tile([P, PACK, FEATS], BF16, name=name)
            nc.sync.dma_start(
                out=raw[:].rearrange("p (u e) h -> p u e h", u=2),
                in_=src[K_PASS * g : K_PASS * (g + 1), :].rearrange("(u p e) h -> p u e h", u=2, e=2),
            )
            return raw

        bias_rows = keep.tile([H_TILES, P], BF16)
        nc.scalar.dma_start(out=bias_rows[:], in_=bias_gate.rearrange("o (j m) -> (o j) m", m=P))

        x_rows = [load_rows(x_in, 0, "x_rows0")]
        raw_weights = [load_weights(w2, 0, "raw_w2_0")]
        state_rows = [load_rows(state, 0, "state_rows0")]
        raw_weights += [
            load_weights(w2, 1, "raw_w2_1"),
            load_weights(u2, 0, "raw_u2_0"),
            load_weights(u2, 1, "raw_u2_1"),
        ]
        cand_rows = [load_rows(cand, 0, "cand_rows0")]
        x_rows.append(load_rows(x_in, 1, "x_rows1"))
        state_rows.append(load_rows(state, 1, "state_rows1"))
        cand_rows.append(load_rows(cand, 1, "cand_rows1"))

        ident = keep.tile([P, P], F32)
        make_identity(nc, ident[:])

        warm = keep.tile([P, 1], F32)
        nc.vector.memset(warm[:], 0.0)
        nc.scalar.activation(out=warm[:], in_=warm[:], func=ACT.Sigmoid)

        bias_square = keep.tile([P, P], F32)
        nc.vector.memset(bias_square[:], 0.0)
        nc.vector.tensor_copy(out=bias_square[0:H_TILES, :], in_=bias_rows[:])
        bias_bank = psum.tile([P, HALF], F32, tag="bank")
        nc.tensor.transpose(bias_bank[:, 0:P], bias_square[:], ident[:])
        bias_col = keep.tile([P, H_TILES], F32)
        nc.vector.tensor_copy(out=bias_col[:], in_=bias_bank[:, 0:H_TILES])

        row_codes = keep.tile([P, PASSES, HALVES, HALF], U32, align_bytes=256)
        row_scales = keep.tile([P, PASSES, HALVES, HALF], U8, align_bytes=256)
        weight_codes = keep.tile([P, PASSES, FEATS], U32, align_bytes=256)
        weight_scales = keep.tile([P, PASSES, FEATS], U8, align_bytes=256)

        def quantise_rows(half, rows, first_pass):
            words_in = rows[:].bitcast(F32)
            grouped = []
            for g in range(2):
                grouped.append(stage.tile([P, PACK * HALF], BF16, tag="grouped", name="grouped%d" % g, align_bytes=64))
            for two in range(2):
                for g in range(2):
                    bank = psum.tile([P, 2, 2 * P], F32, tag="bank")
                    for u in range(2):
                        for ii in range(2):
                            first = (K_PASS // 2) * g + P * u
                            nc.tensor.transpose(
                                bank[:, u, P * ii : P * (ii + 1)],
                                words_in[:, 2 * two + ii, first : first + P],
                                ident[:],
                            )
                    words_out = grouped[g][:].bitcast(F32).rearrange("q (n u) -> q n u", u=2)
                    nc.scalar.copy(
                        out=words_out[:, 2 * P * two : 2 * P * (two + 1), :],
                        in_=bank[:].rearrange("q u n -> q n u"),
                    )
            for g in range(2):
                nc.vector.quantize_mx(
                    out=row_codes[:, first_pass + g, half, :].bitcast(FP8X4),
                    scales=row_scales[:, first_pass + g, half, :],
                    in_=grouped[g][:],
                )

        def quantise_weights(c):
            for part in range(2):
                cols = slice(HALF * part, HALF * (part + 1))
                grouped = stage.tile([P, PACK * HALF], BF16, tag="grouped", align_bytes=64)
                dst = grouped[:].rearrange("p (a i t) -> p a t i", i=4, t=PACK)
                src = raw_weights[c][:, :, cols].rearrange("p t (a i) -> p a t i", i=4)
                if part == 0:
                    nc.vector.tensor_copy(out=dst, in_=src)
                else:
                    nc.scalar.copy(out=dst, in_=src)
                nc.vector.quantize_mx(
                    out=weight_codes[:, c, cols].bitcast(FP8X4),
                    scales=weight_scales[:, c, cols],
                    in_=grouped[:],
                )

        def mx_pass(acc, c, half, j, cols=slice(0, HALF)):
            h_cols = slice(P * j, P * (j + 1))
            nc.tensor.matmul_mx(
                out=acc[:],
                lhsT=weight_codes[:, c, h_cols].bitcast(FP8X4),
                lhsT_scale=weight_scales[:, c, h_cols],
                rhs=row_codes[:, c, half, cols].bitcast(FP8X4),
                rhs_scale=row_scales[:, c, half, cols],
                start=(c == 0),
                stop=(c == PASSES - 1),
            )

        def gate(acc, j):
            z_t = gates.tile([P, HALF], F32, tag="z_t")
            nc.scalar.activation(out=z_t[:], in_=acc[:], func=ACT.Sigmoid, bias=bias_col[:, j : j + 1], scale=1.0)
            return z_t

        def blend_tile(z_t, half, j, result, last_engine):
            z = psum.tile([P, ROWS_PER_PART, P], F32, tag="bank")
            for i in range(ROWS_PER_PART):
                nc.tensor.transpose(z[:, i, :], z_t[:, P * i : P * (i + 1)], ident[:])
            h_cols = slice(P * j, P * (j + 1))
            kept = blend.tile([P, ROWS_PER_PART, P], F32, tag="kept")
            if (half, j) in spans:
                nc.vector.tensor_tensor(out=kept[:], in0=z[:], in1=spans[half, j][:], op=ALU.mult)
                last_engine.tensor_tensor(out=result, in0=kept[:], in1=cand_rows[half][:, :, h_cols], op=ALU.add)
                return
            nc.vector.tensor_tensor(out=kept[:], in0=z[:], in1=state_rows[half][:, :, h_cols], op=ALU.mult)
            fresh = blend.tile([P, ROWS_PER_PART, P], F32, tag="fresh")
            nc.vector.scalar_tensor_tensor(
                out=fresh[:], in0=z[:], scalar=-1.0, in1=cand_rows[half][:, :, h_cols], op0=ALU.add, op1=ALU.mult
            )
            last_engine.tensor_tensor(out=result, in0=kept[:], in1=fresh[:], op=ALU.subtract)

        quantise_weights(0)
        quantise_rows(0, x_rows[0], 0)
        quantise_weights(1)
        quantise_rows(0, state_rows[0], 2)

        spans = {}
        for j in SPAN_TILES:
            h_cols = slice(P * j, P * (j + 1))
            span = keep.tile([P, ROWS_PER_PART, P], F32, name="span%d" % j)
            nc.gpsimd.tensor_tensor(
                out=span[:], in0=state_rows[0][:, :, h_cols], in1=cand_rows[0][:, :, h_cols], op=ALU.subtract
            )
            spans[0, j] = span

        first_acc = []
        for j in range(H_TILES):
            first_acc.append(psum.tile([P, HALF], F32, tag="bank", name="first_acc%d" % j))
        for c in range(PASSES):
            if c >= 2:
                quantise_weights(c)
            for j in range(H_TILES):
                mx_pass(first_acc[j], c, 0, j)
        def blend_pair(z_pair, half, j):
            result = blend.tile([P, ROWS_PER_PART, PAIR * P], F32, tag="result")
            for k in range(PAIR):
                blend_tile(z_pair[k], half, j + k, result[:, :, P * k : P * (k + 1)], nc.gpsimd)
            nc.sync.dma_start(
                out=out[HALF * half : HALF * (half + 1), P * j : P * (j + PAIR)].rearrange(
                    "(p i) h -> p i h", i=ROWS_PER_PART
                ),
                in_=result[:],
            )

        def blend_single(z_t, half, j, last_engine):
            result = blend.tile([P, ROWS_PER_PART, P], F32, tag="single")
            blend_tile(z_t, half, j, result[:], last_engine)
            nc.sync.dma_start(
                out=out[HALF * half : HALF * (half + 1), P * j : P * (j + 1)].rearrange(
                    "(p i) h -> p i h", i=ROWS_PER_PART
                ),
                in_=result[:],
            )

        first_z = [gate(first_acc[j], j) for j in range(H_TILES)]

        blend_pair(first_z[0:2], 0, 0)
        blend_pair(first_z[2:4], 0, 2)
        quantise_rows(1, x_rows[1], 0)
        blend_pair(first_z[4:6], 0, 4)
        quantise_rows(1, state_rows[1], 2)
        blend_pair(first_z[6:8], 0, 6)

        def last_gate(part):
            j = H_TILES - 1
            part_acc = psum.tile([P, 2 * P], F32, tag="bank")
            for c in range(PASSES):
                mx_pass(part_acc, c, 1, j, slice(2 * P * part, 2 * P * (part + 1)))
            z_part = gates.tile([P, 2 * P], F32, tag="z_part")
            nc.scalar.activation(
                out=z_part[:], in_=part_acc[:], func=ACT.Sigmoid, bias=bias_col[:, j : j + 1], scale=1.0
            )
            return z_part

        def last_blend(z_part, part):
            h_cols = slice(P * (H_TILES - 1), P * H_TILES)
            rows = slice(2 * part, 2 * part + 2)
            z = psum.tile([P, 2, P], F32, tag="bank")
            for i in range(2):
                nc.tensor.transpose(z[:, i, :], z_part[:, P * i : P * (i + 1)], ident[:])
            kept = blend.tile([P, 2, P], F32, tag="kept")
            nc.vector.tensor_tensor(out=kept[:], in0=z[:], in1=last_span[:, rows, :], op=ALU.mult)
            result = blend.tile([P, 2, P], F32, tag="part")
            nc.vector.tensor_tensor(out=result[:], in0=kept[:], in1=cand_rows[1][:, rows, h_cols], op=ALU.add)
            nc.sync.dma_start(
                out=out[HALF:ROWS, h_cols].rearrange("(p i) h -> p i h", i=ROWS_PER_PART)[:, rows, :], in_=result[:]
            )

        second_z = []
        early_acc = []
        for j in range(EARLY):
            early_acc.append(psum.tile([P, HALF], F32, tag="bank", name="early_acc%d" % j))
            for c in range(2):
                mx_pass(early_acc[j], c, 1, j)
        for j in range(H_TILES - 1):
            if j < EARLY:
                acc = early_acc[j]
                passes = range(2, PASSES)
            else:
                acc = psum.tile([P, HALF], F32, tag="bank")
                passes = range(PASSES)
            for c in passes:
                mx_pass(acc, c, 1, j)
            second_z.append(gate(acc, j))
            if j % PAIR == 1 and j >= 2 * PAIR - 1:
                blend_pair(second_z[j - 3 : j - 1], 1, j - 3)
        for j in range(H_TILES - 2 * PAIR, H_TILES - PAIR):
            blend_single(second_z[j], 1, j, nc.gpsimd)
        last_cols = slice(P * (H_TILES - 1), P * H_TILES)
        last_span = keep.tile([P, ROWS_PER_PART, P], F32)
        nc.vector.tensor_tensor(
            out=last_span[:], in0=state_rows[1][:, :, last_cols], in1=cand_rows[1][:, :, last_cols], op=ALU.subtract
        )
        last_z = [last_gate(part) for part in range(2)]
        blend_single(second_z[H_TILES - 2], 1, H_TILES - 2, nc.vector)
        for part in range(2):
            last_blend(last_z[part], part)
